import numpy as np
import ml_dtypes


def mxq(x, axis, fmt="e4m3"):
    dtype, down = {"e4m3": (ml_dtypes.float8_e4m3fn, 7), "e5m2": (ml_dtypes.float8_e5m2, 14)}[fmt]
    v = np.moveaxis(np.asarray(x, np.float32).astype(ml_dtypes.bfloat16).astype(np.float64), axis, -1)
    blocks = v.reshape(v.shape[:-1] + (-1, 32))
    amax = np.abs(blocks).max(-1, keepdims=True)
    byte = np.maximum(np.where(amax > 0, np.frexp(amax)[1] - 1 + 127, 0) - down, 1)
    scale = np.exp2(byte - 127.0)
    codes = (blocks / scale).astype(np.float32).astype(dtype).astype(np.float64)
    return np.moveaxis((codes * scale).reshape(v.shape), -1, axis)


WIDE = False


def mx_kscale(k):
    if not WIDE:
        return np.ones(k)
    levels = np.array([10, -10, 5, -5, 0])
    if k % 512:
        return np.exp2(np.random.permutation(np.resize(levels, k // 32))).repeat(32)
    a = np.empty((k // 512, 16))
    for p in range(k // 512):
        a[p, :8] = np.random.permutation(np.resize(levels, 8))
        for g in range(8):
            far = levels[np.abs(levels - a[p, g]) >= 10]
            a[p, g + 8] = far[np.random.randint(len(far))]
    return np.exp2(a.ravel()).repeat(32)


BF16 = ml_dtypes.bfloat16


def bf(x):
    return np.asarray(x, np.float32).astype(BF16)


def f64(x):
    return np.asarray(x).astype(np.float64)


T, B, I, H = 16, 128, 512, 1024


def sigmoid(v):
    return 1.0 / (1.0 + np.exp(-v))


def setup_inputs():
    s = mx_kscale(I)
    return {"input_seq": bf(np.random.standard_normal((T, B, I)) * s),
            "W_ih": bf(np.random.standard_normal((3 * H, I)) / np.sqrt(I) / s[None, :]),
            "b_ih": bf(np.random.standard_normal(3 * H) * 0.3),
            "gh": bf(np.random.standard_normal((B, 3 * H)) * 0.5)}


def core(input_seq, W_ih, b_ih, gh):
    gi = (mxq(f64(input_seq), 2, "e4m3") @ mxq(f64(W_ih), 1, "e4m3").T) + f64(b_ih)
    g = f64(gh)
    i_r, i_z, i_n = gi[..., :H], gi[..., H:2 * H], gi[..., 2 * H:]
    h_r, h_z, h_n = g[..., :H], g[..., H:2 * H], g[..., 2 * H:]
    r = sigmoid(i_r + h_r)
    z = sigmoid(i_z + h_z)
    n = np.tanh(i_n + r * h_n)
    h = (1.0 - z) * n
    return np.transpose(h, (1, 0, 2))


def e4m3fn_bytes(y):
    return np.clip(np.asarray(y, np.float64), -448.0, 448.0).astype(np.float32).astype(ml_dtypes.float8_e4m3fn).view(np.uint8)


def reference(input_seq, W_ih, b_ih, gh):
    out = core(input_seq, W_ih, b_ih, gh)
    s = np.max(np.abs(out), axis=-1, keepdims=True) / 448.0
    return out, e4m3fn_bytes(out / s)

@@ -1,0 +1,581 @@
+from contextlib import ExitStack
+
+import concourse.mybir as mybir
+from concourse.masks import make_identity
+
+T, B, I, H = 16, 128, 512, 1024
+FLOPS = 2 * T * B * I * 3 * H
+
+F32 = mybir.dt.float32
+BF16 = mybir.dt.bfloat16
+U32 = mybir.dt.uint32
+U8 = mybir.dt.uint8
+FP8X4 = mybir.dt.float8_e4m3fn_x4
+FP8 = mybir.dt.float8_e4m3fn
+ACT = mybir.ActivationFunctionType
+ALU = mybir.AluOpType
+AX = mybir.AxisListType
+
+P = 128
+TG = 4
+NTG = T // TG
+NJ = H // P
+R_BUFS, Z_BUFS, N_BUFS, TP_BUFS = 1, 1, 1, 5
+D1 = 4
+DZ = 3
+BUDGET_V = 4.2
+BUDGET_S = 4.2
+AMAX_SLACK = 8
+CAST_SLACK = 12
+LEAD = 4
+AMAX_LAG = 2
+DRAIN_V = 4.2
+DRAIN_S = 4.2
+
+
+def chunk_list():
+    chunks = [[(0, 0)], [(0, 1)], [(1, 0), (1, 1)]]
+    for j in range(2, NJ):
+        chunks.append([(0, j), (1, j)])
+    for j in range(0, NJ, 2):
+        chunks.append([(2, j), (2, j + 1)])
+    for j in range(0, NJ - 2, 2):
+        chunks.append([(3, j), (3, j + 1)])
+    chunks.append([(3, NJ - 2)])
+    chunks.append([(3, NJ - 1)])
+    return chunks
+
+
+def tile_grucellmodel_pa_kernel(tc, input_seq, W_ih, b_ih, gh, out_0, out_1):
+    nc = tc.nc
+    chunks = chunk_list()
+    NC = len(chunks)
+    with ExitStack() as ctx:
+        ctx.enter_context(tc.manual_schedule())
+        const = ctx.enter_context(tc.tile_pool(name="const", bufs=1))
+        stage = ctx.enter_context(tc.tile_pool(name="stage", bufs=3))
+        work = ctx.enter_context(tc.tile_pool(name="work", bufs=2))
+        psum = ctx.enter_context(tc.psum_pool(name="psum", bufs=1))
+
+        b_rows = const.tile([P, P], BF16, name="b_rows", tag="b_rows")
+        nc.gpsimd.memset(b_rows[:], 0.0)
+        ident_f = const.tile([P, P], F32, name="ident_f", tag="ident_f")
+        make_identity(nc, ident_f[:])
+        ident_b = const.tile([P, P], BF16, name="ident_b", tag="ident_b")
+        make_identity(nc, ident_b[:])
+        zero = const.tile([P, 1], F32, name="zero", tag="zero")
+        nc.vector.memset(zero[:], 0.0)
+        warm = const.tile([P, 1], F32, name="warm", tag="warm")
+        nc.scalar.activation(out=warm[:], in_=zero[:], func=ACT.Sigmoid)
+
+        raw = {}
+        gh_raw = {}
+        w_view = W_ih.rearrange("(g j p) k -> p g j k", g=3, j=NJ)
+        gh_view = gh.rearrange("b (g j c) -> b g j c", g=3, j=NJ)
+
+        def load(key, shape, src, tag, bufs):
+            t_ = const.tile(shape, BF16, name=tag, tag=tag, bufs=bufs)
+            nc.sync.dma_start(out=t_[:], in_=src)
+            raw[key] = t_
+
+        def load_x(tg):
+            load(("x", tg), [P, TG, I], input_seq[TG * tg:TG * (tg + 1)].rearrange("t b k -> b t k"), "raw_x", 2)
+
+        def load_rz(j):
+            load(("rz", j), [P, 2, I], w_view[:, 0:2, j, :], "raw_rz%d" % j, 1)
+
+        def load_n(u):
+            load(("n", u), [P, 4, I], w_view[:, 2, 4 * u:4 * u + 4, :], "raw_n%d" % u, 1)
+
+        def load_gh(hh):
+            t_ = const.tile([P, 3, 4, P], BF16, name="gh_raw%d" % hh, tag="gh_raw%d" % hh)
+            nc.sync.dma_start(out=t_[:], in_=gh_view[:, :, 4 * hh:4 * hh + 4, :])
+            gh_raw[hh] = t_
+
+        load_x(0)
+        load_rz(0)
+        load_rz(1)
+        load_gh(0)
+        nc.sync.dma_start(out=b_rows[0:24, :], in_=b_ih.rearrange("(c p) -> c p", p=P))
+        load_n(0)
+        load_x(1)
+        load_rz(2)
+        load_rz(3)
+        load_rz(4)
+        load_rz(5)
+        load_gh(1)
+        load_n(1)
+        load_rz(6)
+        load_rz(7)
+
+        turned = {}
+        grouped = {}
+        codes = {}
+        scales = {}
+
+        def copy(eng, out, in_):
+            if eng == "v":
+                nc.vector.tensor_copy(out=out, in_=in_)
+            else:
+                nc.scalar.copy(out=out, in_=in_)
+
+        def source(kind, u, c):
+            if kind == "rz":
+                return raw[("rz", 2 * u + c // 2)][:, c % 2, :].bitcast(F32)
+            return raw[(kind, u)][:, c, :].bitcast(F32)
+
+        def where(j, g):
+            if g < 2:
+                return ("rz", j // 2), (j % 2) * 2 + g
+            return ("n", j // 4), j % 4
+
+        def turn(kind, u):
+            banks = []
+            for hb in range(2):
+                pt = psum.tile([P, 2, 2, P], F32, name="tp", tag="tp", bufs=TP_BUFS)
+                for a in range(2):
+                    for w in range(2):
+                        nc.tensor.transpose(pt[:, a, w, :], source(kind, u, 2 * hb + a)[:, w:I // 2:2], ident_f[:])
+                banks.append(pt)
+            turned[(kind, u)] = banks
+
+        def gather(kind, u, hb, eng):
+            if hb == 0:
+                grouped[(kind, u)] = stage.tile([P, 4 * I], BF16, name="grouped", tag="grouped", align_bytes=64)
+            g_ = grouped[(kind, u)]
+            dst = g_[:, 2 * I * hb:2 * I * (hb + 1)].bitcast(F32).rearrange("p (a r w) -> p a r w", a=2, w=2)
+            src = turned[(kind, u)][hb][:].rearrange("p a w r -> p a r w")
+            copy(eng, dst, src)
+
+        def quant(kind, u, halves):
+            key = (kind, u)
+            if key not in codes:
+                name = "%s%d" % key
+                codes[key] = const.tile([P, 4 * P], U32, name="codes_" + name, tag="codes_" + name, align_bytes=64)
+                scales[key] = const.tile([P, 4 * P], U8, name="scales_" + name, tag="scales_" + name, align_bytes=64)
+            lo, hi = 2 * P * halves[0], 2 * P * (halves[-1] + 1)
+            nc.vector.quantize_mx(
+                out=codes[key][:, lo:hi].bitcast(FP8X4), scales=scales[key][:, lo:hi], in_=grouped[key][:, 4 * lo:4 * hi]
+            )
+
+        gh_ps = {}
+        ghT = {}
+        for kind in ("r", "z", "n"):
+            ghT[kind] = const.tile([P, NJ, 1, P], F32, name="ghT_" + kind, tag="ghT_" + kind)
+        bias = const.tile([P, 24, 1], F32, name="bias", tag="bias")
+        b_ps = {}
+
+        def gh_turn(kind, u):
+            if kind == "z":
+                pt = psum.tile([P, 4, P], F32, name="tp", tag="tp", bufs=TP_BUFS)
+                for c in range(4):
+                    row = NJ + 4 * u + c
+                    nc.tensor.matmul(out=pt[:, c, :], lhsT=ident_b[:], rhs=gh_raw[u][:, 1, c, :], start=True, stop=False)
+                    nc.tensor.matmul(
+                        out=pt[:, c, :], lhsT=ident_b[:, row:row + 1].to_broadcast([P, P]), rhs=b_rows[:],
+                        start=False, stop=True,
+                    )
+            else:
+                pt = psum.tile([P, 4, P], BF16, name="tp", tag="tp", bufs=TP_BUFS)
+                for c in range(4):
+                    nc.tensor.transpose(pt[:, c, :], gh_raw[u][:, 0 if kind == "r" else 2, c, :], ident_b[:])
+            gh_ps[(kind, u)] = pt
+
+        def gh_gather(kind, u, eng):
+            dst = ghT[kind][:, 4 * u:4 * u + 4, 0, :]
+            if kind == "r":
+                nc.vector.tensor_tensor(
+                    out=dst, in0=gh_ps[(kind, u)][:], in1=bias[:, 4 * u:4 * u + 4, :].to_broadcast([P, 4, P]), op=ALU.add
+                )
+            else:
+                copy(eng, dst, gh_ps[(kind, u)][:])
+
+        def bias_turn():
+            pt = psum.tile([P, P], BF16, name="tp", tag="tp", bufs=TP_BUFS)
+            nc.tensor.transpose(pt[:], b_rows[:], ident_b[:])
+            b_ps[0] = pt
+
+        def bias_gather():
+            nc.vector.tensor_copy(out=bias[:, :, 0], in_=b_ps[0][:, 0:24])
+
+        acc = {}
+        sb = {}
+        o_t = {}
+        f8_t = {}
+        part = {}
+        rs_t = {}
+
+        def steps(K):
+            return list(enumerate(chunks[K])) if 0 <= K < NC else []
+
+        def mm(K, g, only=None):
+            for pos, (tg, j) in steps(K):
+                if only is not None and pos != only:
+                    continue
+                key, c = where(j, g)
+                tag = "acc%d" % g
+                ps = psum.tile([P, TG, P], F32, name=tag, tag=tag, bufs=(R_BUFS, Z_BUFS, N_BUFS)[g])
+                cols = slice(c * P, (c + 1) * P)
+                if g == 1:
+                    for t in range(TG):
+                        rows = slice(t * P, (t + 1) * P)
+                        nc.tensor.matmul_mx(
+                            out=ps[:, t, :],
+                            lhsT=codes[("x", tg)][:, rows].bitcast(FP8X4),
+                            lhsT_scale=scales[("x", tg)][:, rows],
+                            rhs=codes[key][:, cols].bitcast(FP8X4),
+                            rhs_scale=scales[key][:, cols],
+                            start=True,
+                            stop=True,
+                        )
+                else:
+                    nc.tensor.matmul_mx(
+                        out=ps[:].rearrange("p t b -> p (t b)"),
+                        lhsT=codes[key][:, cols].bitcast(FP8X4),
+                        lhsT_scale=scales[key][:, cols],
+                        rhs=codes[("x", tg)][:].bitcast(FP8X4),
+                        rhs_scale=scales[("x", tg)][:],
+                        start=True,
+                        stop=True,
+                    )
+                acc[(K, pos, g)] = ps
+
+        def wide(what, K, bufs):
+            if (what, K) not in sb:
+                sb[(what, K)] = work.tile([P, 2, TG, P], F32, name=what, tag=what, bufs=bufs)
+            return sb[(what, K)]
+
+        def add_gh(K, pos, g):
+            tg, j = chunks[K][pos]
+            kind = ("r", "z")[g]
+            t_ = wide("a" + kind, K, 2)
+            nc.vector.tensor_tensor(
+                out=t_[:, pos], in0=acc[(K, pos, g)][:], in1=ghT[kind][:, j, :, :].to_broadcast([P, TG, P]), op=ALU.add
+            )
+
+        def sig(K, kind):
+            if not steps(K):
+                return
+            n = len(chunks[K])
+            t_ = wide(kind, K, 3 if kind == "z" else 2)
+            nc.scalar.activation(
+                out=t_[:, 0:n], in_=sb[("a" + kind, K)][:, 0:n], func=ACT.Sigmoid, scale=(1.0 if kind == "r" else -1.0)
+            )
+
+        def mul_m(K):
+            if not steps(K):
+                return
+            ch = chunks[K]
+            n = len(ch)
+            t_ = wide("m", K, 3)
+            if n == 2 and ch[0][1] != ch[1][1]:
+                in1 = ghT["n"][:, ch[0][1]:ch[0][1] + 2, :, :].to_broadcast([P, 2, TG, P])
+            else:
+                in1 = ghT["n"][:, ch[0][1]:ch[0][1] + 1, :, :].to_broadcast([P, n, TG, P])
+            nc.gpsimd.tensor_tensor(out=t_[:, 0:n], in0=sb[("r", K)][:, 0:n], in1=in1, op=ALU.mult)
+
+        def add_n(K, pos):
+            tg, j = chunks[K][pos]
+            t_ = work.tile([P, TG, P], F32, name="np", tag="np", bufs=3)
+            nc.vector.scalar_tensor_tensor(
+                out=t_[:], in0=acc[(K, pos, 2)][:], scalar=bias[:, 2 * NJ + j, :], in1=sb[("m", K)][:, pos],
+                op0=ALU.add, op1=ALU.add,
+            )
+            sb[("np", K, pos)] = t_
+
+        def turn_np(K, pos):
+            pt = psum.tile([P, TG, P], F32, name="tp", tag="tp", bufs=TP_BUFS)
+            for t in range(TG):
+                nc.tensor.transpose(pt[:, t, :], sb[("np", K, pos)][:, t, :], ident_f[:])
+            acc[(K, pos, 3)] = pt
+
+        def gate_n(K, pos):
+            t_ = wide("n", K, 2)
+            nc.scalar.activation(out=t_[:, pos], in_=acc[(K, pos, 3)][:], func=ACT.Tanh)
+
+        done = {}
+
+        def mul_h(K):
+            if not steps(K):
+                return
+            ch = chunks[K]
+            n = len(ch)
+            tg, j = ch[0]
+            hf = tg // 2
+            if hf not in o_t:
+                o_t[hf] = const.tile([P, 2 * TG, H], F32, name="o%d" % hf, tag="o%d" % hf)
+            row = TG * (tg % 2)
+            zc, n_ = sb[("z", K)], sb[("n", K)]
+            if n == 2 and ch[1][0] != tg:
+                dst = o_t[hf][:, :, j * P:(j + 1) * P]
+                nc.gpsimd.tensor_tensor(
+                    out=dst, in0=zc[:].rearrange("p n t c -> p (n t) c"), in1=n_[:].rearrange("p n t c -> p (n t) c"), op=ALU.mult
+                )
+            elif n == 2:
+                dst = o_t[hf][:, row:row + TG, j * P:(j + 2) * P].rearrange("p t (n c) -> p n t c", n=2)
+                nc.gpsimd.tensor_tensor(out=dst, in0=zc[:], in1=n_[:], op=ALU.mult)
+            else:
+                dst = o_t[hf][:, row:row + TG, j * P:(j + 1) * P]
+                nc.gpsimd.tensor_tensor(out=dst, in0=zc[:, 0], in1=n_[:, 0], op=ALU.mult)
+            for tg_, j_ in ch:
+                done[tg_] = done.get(tg_, 0) + 1
+                bd = bounds(tg_)
+                cols = done[tg_] * P
+                if tg_ == NTG - 1:
+                    if cols in bd:
+                        store_o(tg_, bd[bd.index(cols) - 1], cols)
+                elif cols == H:
+                    store_o(tg_, 0, H)
+
+        def rows_of(tg):
+            return o_t[tg // 2][:, TG * (tg % 2):TG * (tg % 2) + TG, :]
+
+        def bounds(tg):
+            if tg == NTG - 1:
+                return [0, 512, 768, 896, 1024]
+            return [0, 512, 1024]
+
+        def amax_piece(tg, s, t):
+            bd = bounds(tg)
+            if tg not in part:
+                part[tg] = const.tile([P, TG, len(bd) - 1], F32, name="part%d" % tg, tag="part%d" % tg)
+            nc.vector.tensor_reduce(
+                out=part[tg][:, t, s:s + 1], in_=rows_of(tg)[:, t, bd[s]:bd[s + 1]], axis=AX.X, op=ALU.max,
+                apply_absolute_value=True,
+            )
+
+        def combine(tg):
+            am = const.tile([P, TG], F32, name="am%d" % tg, tag="am%d" % tg)
+            rc = const.tile([P, TG], F32, name="rc%d" % tg, tag="rc%d" % tg)
+            rs = const.tile([P, TG], F32, name="rs%d" % tg, tag="rs%d" % tg)
+            nc.vector.tensor_reduce(out=am[:], in_=part[tg][:], axis=AX.X, op=ALU.max)
+            nc.vector.reciprocal(out=rc[:], in_=am[:])
+            nc.vector.tensor_scalar(out=rs[:], in0=rc[:], scalar1=448.0, scalar2=None, op0=ALU.mult)
+            rs_t[tg] = rs
+            f8_t[tg] = const.tile([P, TG, H], FP8, name="f8_%d" % tg, tag="f8_%d" % tg)
+
+        def cast_piece(tg, t, c0, c1, eng):
+            if eng == "s":
+                nc.scalar.activation(
+                    out=f8_t[tg][:, t, c0:c1], in_=rows_of(tg)[:, t, c0:c1], func=ACT.Identity,
+                    scale=rs_t[tg][:, t:t + 1], bias=zero[:, 0:1], saturate=False,
+                )
+            else:
+                nc.vector.tensor_scalar(
+                    out=f8_t[tg][:, t, c0:c1], in0=rows_of(tg)[:, t, c0:c1], scalar1=rs_t[tg][:, t:t + 1],
+                    scalar2=None, op0=ALU.mult, saturate=False,
+                )
+
+        def store_o(tg, c0, c1):
+            nc.sync.dma_start(out=out_0[:, TG * tg:TG * (tg + 1), c0:c1], in_=rows_of(tg)[:, :, c0:c1])
+
+        def store_f8(tg, t0, t1):
+            nc.sync.dma_start(out=out_1[:, TG * tg + t0:TG * tg + t1, :], in_=f8_t[tg][:, t0:t1, :].bitcast(U8))
+
+        flat = []
+        for K in range(NC):
+            for pos in range(len(chunks[K])):
+                flat.append((K, pos))
+        NS = len(flat)
+
+        def ok(i):
+            return 0 <= i < NS
+
+        def last(i):
+            return ok(i) and flat[i][1] == len(chunks[flat[i][0]]) - 1
+
+        first_use = {}
+        h_iter = {}
+        cnt = {}
+        for i in range(NS):
+            K, pos = flat[i]
+            tg, j = chunks[K][pos]
+            for key in (("x", tg), ("rz", j // 2), ("n", j // 4), ("gr", j // 4), ("gz", j // 4), ("gn", j // 4)):
+                first_use.setdefault(key, i)
+            cnt[tg] = cnt.get(tg, 0) + P
+            h_iter[(tg, cnt[tg])] = i + (len(chunks[K]) - 1 - pos) + D1 + 1
+        LAST = NS + D1
+
+        tasks = []
+        count = {"n": 0}
+        left = {}
+        load_now = {"v": 0.0, "s": 0.0}
+        credit = {"v": 0.0, "s": 0.0}
+
+        def queue(due, ready, what, *args):
+            count["n"] += 1
+            tasks.append([due, count["n"], ready, what, args])
+
+        for tg in range(NTG):
+            bd = bounds(tg)
+            left[("amax", tg)] = TG * (len(bd) - 1)
+            for s in range(len(bd) - 1):
+                ready = min(h_iter[(tg, bd[s + 1])] + AMAX_LAG, LAST)
+                for t in range(TG):
+                    queue(ready + (0 if tg == NTG - 1 else AMAX_SLACK), ready, "amax", tg, s, t)
+
+        def cost_of(what, args, eng):
+            if what == "amax":
+                bd = bounds(args[0])
+                return (bd[args[1] + 1] - bd[args[1]]) / 512.0
+            if what == "combine":
+                return 0.5
+            if what == "cast":
+                return (args[3] - args[2]) / (1024.0 if eng == "v" else 512.0)
+            return 1.0
+
+        def engines_of(what, args, i):
+            if what in ("amax", "combine", "quant") or (what == "ghg" and args[0] == "r"):
+                return ["v"]
+            if what == "cast":
+                return ["s", "v"] if i >= LAST else ["s"]
+            if what == "gather":
+                return ["s"] if i >= 2 else ["s", "v"]
+            return ["s", "v"]
+
+        def emit(what, args, eng, i):
+            nxt = i if i >= LAST else i + 1
+            if what == "gather":
+                kind, u, hb, due = args
+                gather(kind, u, hb, eng)
+                left[(kind, u)] -= 1
+                if left[(kind, u)] == 0:
+                    queue(max(due, i + 1), i + 1, "quant", kind, u)
+            elif what == "quant":
+                quant(args[0], args[1], [0, 1])
+            elif what == "ghg":
+                gh_gather(args[0], args[1], eng)
+            elif what == "amax":
+                amax_piece(*args)
+                tg = args[0]
+                left[("amax", tg)] -= 1
+                if left[("amax", tg)] == 0:
+                    queue(nxt, nxt, "combine", tg)
+            elif what == "combine":
+                tg = args[0]
+                combine(tg)
+                for t in range(TG):
+                    if tg == NTG - 1:
+                        queue(nxt, nxt, "cast", tg, t, 0, 512)
+                        queue(nxt, nxt, "cast", tg, t, 512, H)
+                    else:
+                        queue(nxt + CAST_SLACK, nxt, "cast", tg, t, 0, H)
+            elif what == "cast":
+                tg, t, c0, c1 = args
+                cast_piece(tg, t, c0, c1, eng)
+                if c1 == H:
+                    if tg >= NTG - 2:
+                        store_f8(tg, t, t + 1)
+                    elif t == TG - 1:
+                        store_f8(tg, 0, TG)
+
+        def side(i):
+            budget = {"v": BUDGET_V, "s": BUDGET_S}
+            if i >= NS:
+                budget = {"v": DRAIN_V, "s": DRAIN_S}
+            if i >= LAST:
+                budget = {"v": 100.0, "s": 100.0}
+            again = True
+            while again:
+                again = False
+                for task in sorted(tasks, key=lambda task: (task[0] if i < LAST else 0, task[1])):
+                    due, number, ready, what, args = task
+                    if ready > i:
+                        continue
+                    best = None
+                    for eng in engines_of(what, args, i):
+                        over = load_now[eng] + cost_of(what, args, eng) - budget[eng] - credit[eng]
+                        if best is None or over < best[0]:
+                            best = (over, eng)
+                    if best[0] > 0 and due > i:
+                        continue
+                    tasks.remove(task)
+                    load_now[best[1]] += cost_of(what, args, best[1])
+                    emit(what, args, best[1], i)
+                    again = True
+                    break
+            for eng in ("v", "s"):
+                credit[eng] = max(-2.0, min(2.0, credit[eng] + budget[eng] - load_now[eng]))
+
+        lag = {"x": -1, "rz": -1, "n": D1 - 1, "gr": -1, "gz": DZ - 1, "gn": -1}
+        need = {}
+        for key in first_use:
+            need[key] = first_use[key] + lag[key[0]]
+        units = sorted(
+            [key for key in first_use if key not in (("x", 0), ("rz", 0), ("gr", 0), ("gz", 0), ("gn", 0))],
+            key=lambda key: (need[key], key),
+        )
+
+        def turns(i):
+            big = 0
+            small = 0
+            for key in list(units):
+                is_gh = key[0] in ("gr", "gz", "gn")
+                forced = need[key] - (1 if is_gh else 2) <= i
+                if not forced and (need[key] - LEAD > i or (small if is_gh else big)):
+                    continue
+                units.remove(key)
+                if is_gh:
+                    small += 1
+                    gh_turn(key[0][1], key[1])
+                    queue(i + 1, i + 1, "ghg", key[0][1], key[1])
+                else:
+                    big += 1
+                    turn(key[0], key[1])
+                    if key == ("x", 1):
+                        load_x(3)
+                    left[key] = 2
+                    queue(i + 1, i + 1, "gather", key[0], key[1], 0, max(i + 1, need[key]))
+                    queue(i + 1, i + 1, "gather", key[0], key[1], 1, max(i + 1, need[key]))
+
+        turn("x", 0)
+        load_x(2)
+        turn("rz", 0)
+        gather("x", 0, 0, "v")
+        gather("x", 0, 1, "s")
+        gather("rz", 0, 0, "s")
+        quant("x", 0, [0, 1])
+        gather("rz", 0, 1, "s")
+        bias_turn()
+        gh_turn("r", 0)
+        gh_turn("n", 0)
+        quant("rz", 0, [0])
+        bias_gather()
+        gh_gather("r", 0, "v")
+        gh_gather("n", 0, "s")
+        gh_turn("z", 0)
+        quant("rz", 0, [1])
+        gh_gather("z", 0, "s")
+
+        def at(i, fn, *a):
+            if ok(i):
+                fn(flat[i][0], flat[i][1], *a)
+
+        def mm1(K, pos, g):
+            mm(K, g, pos)
+
+        i = -1
+        while i < LAST + 1 or tasks:
+            load_now["v"] = 1.0 * (ok(i) + ok(i - DZ) + ok(i - D1))
+            load_now["s"] = 1.0 * ok(i - D1 - 1)
+            for e in (i, i - DZ):
+                if last(e):
+                    load_now["s"] += len(chunks[flat[e][0]])
+            at(i - D1 - 1, gate_n)
+            if last(i - D1 - 1):
+                mul_h(flat[i - D1 - 1][0])
+            at(i, add_gh, 0)
+            if last(i):
+                sig(flat[i][0], "r")
+                mul_m(flat[i][0])
+            at(i - DZ, add_gh, 1)
+            if last(i - DZ):
+                sig(flat[i - DZ][0], "z")
+            at(i - D1, add_n)
+            side(i)
+            at(i + 1, mm1, 0)
+            at(i - DZ + 1, mm1, 1)
+            at(i - D1 + 1, mm1, 2)
+            at(i - D1, turn_np)
+            turns(i)
+            i += 1

@@ -51,7 +51,6 @@ def tile_grucellmodel_pa_kernel(tc, input_seq, W_ih, b_ih, gh, out_0, out_1):
     chunks = chunk_list()
     NC = len(chunks)
     with ExitStack() as ctx:
-        ctx.enter_context(tc.manual_schedule())
         const = ctx.enter_context(tc.tile_pool(name="const", bufs=1))
         stage = ctx.enter_context(tc.tile_pool(name="stage", bufs=3))
         work = ctx.enter_context(tc.tile_pool(name="work", bufs=2))

from contextlib import ExitStack

import concourse.mybir as mybir
from concourse.masks import make_identity

T, B, I, H = 16, 128, 512, 1024
FLOPS = 2 * T * B * I * 3 * H

F32 = mybir.dt.float32
BF16 = mybir.dt.bfloat16
U32 = mybir.dt.uint32
U8 = mybir.dt.uint8
FP8X4 = mybir.dt.float8_e4m3fn_x4
FP8 = mybir.dt.float8_e4m3fn
ACT = mybir.ActivationFunctionType
ALU = mybir.AluOpType
AX = mybir.AxisListType

P = 128
TG = 4
NTG = T // TG
NJ = H // P
R_BUFS, Z_BUFS, N_BUFS, TP_BUFS = 1, 1, 1, 5
D1 = 4
DZ = 3
BUDGET_V = 4.2
BUDGET_S = 4.2
AMAX_SLACK = 8
CAST_SLACK = 12
LEAD = 4
AMAX_LAG = 2
DRAIN_V = 4.2
DRAIN_S = 4.2


def chunk_list():
    chunks = [[(0, 0)], [(0, 1)], [(1, 0), (1, 1)]]
    for j in range(2, NJ):
        chunks.append([(0, j), (1, j)])
    for j in range(0, NJ, 2):
        chunks.append([(2, j), (2, j + 1)])
    for j in range(0, NJ - 2, 2):
        chunks.append([(3, j), (3, j + 1)])
    chunks.append([(3, NJ - 2)])
    chunks.append([(3, NJ - 1)])
    return chunks


def tile_grucellmodel_pa_kernel(tc, input_seq, W_ih, b_ih, gh, out_0, out_1):
    nc = tc.nc
    chunks = chunk_list()
    NC = len(chunks)
    with ExitStack() as ctx:
        const = ctx.enter_context(tc.tile_pool(name="const", bufs=1))
        stage = ctx.enter_context(tc.tile_pool(name="stage", bufs=3))
        work = ctx.enter_context(tc.tile_pool(name="work", bufs=2))
        psum = ctx.enter_context(tc.psum_pool(name="psum", bufs=1))

        b_rows = const.tile([P, P], BF16, name="b_rows", tag="b_rows")
        nc.gpsimd.memset(b_rows[:], 0.0)
        ident_f = const.tile([P, P], F32, name="ident_f", tag="ident_f")
        make_identity(nc, ident_f[:])
        ident_b = const.tile([P, P], BF16, name="ident_b", tag="ident_b")
        make_identity(nc, ident_b[:])
        zero = const.tile([P, 1], F32, name="zero", tag="zero")
        nc.vector.memset(zero[:], 0.0)
        warm = const.tile([P, 1], F32, name="warm", tag="warm")
        nc.scalar.activation(out=warm[:], in_=zero[:], func=ACT.Sigmoid)

        raw = {}
        gh_raw = {}
        w_view = W_ih.rearrange("(g j p) k -> p g j k", g=3, j=NJ)
        gh_view = gh.rearrange("b (g j c) -> b g j c", g=3, j=NJ)

        def load(key, shape, src, tag, bufs):
            t_ = const.tile(shape, BF16, name=tag, tag=tag, bufs=bufs)
            nc.sync.dma_start(out=t_[:], in_=src)
            raw[key] = t_

        def load_x(tg):
            load(("x", tg), [P, TG, I], input_seq[TG * tg:TG * (tg + 1)].rearrange("t b k -> b t k"), "raw_x", 2)

        def load_rz(j):
            load(("rz", j), [P, 2, I], w_view[:, 0:2, j, :], "raw_rz%d" % j, 1)

        def load_n(u):
            load(("n", u), [P, 4, I], w_view[:, 2, 4 * u:4 * u + 4, :], "raw_n%d" % u, 1)

        def load_gh(hh):
            t_ = const.tile([P, 3, 4, P], BF16, name="gh_raw%d" % hh, tag="gh_raw%d" % hh)
            nc.sync.dma_start(out=t_[:], in_=gh_view[:, :, 4 * hh:4 * hh + 4, :])
            gh_raw[hh] = t_

        load_x(0)
        load_rz(0)
        load_rz(1)
        load_gh(0)
        nc.sync.dma_start(out=b_rows[0:24, :], in_=b_ih.rearrange("(c p) -> c p", p=P))
        load_n(0)
        load_x(1)
        load_rz(2)
        load_rz(3)
        load_rz(4)
        load_rz(5)
        load_gh(1)
        load_n(1)
        load_rz(6)
        load_rz(7)

        turned = {}
        grouped = {}
        codes = {}
        scales = {}

        def copy(eng, out, in_):
            if eng == "v":
                nc.vector.tensor_copy(out=out, in_=in_)
            else:
                nc.scalar.copy(out=out, in_=in_)

        def source(kind, u, c):
            if kind == "rz":
                return raw[("rz", 2 * u + c // 2)][:, c % 2, :].bitcast(F32)
            return raw[(kind, u)][:, c, :].bitcast(F32)

        def where(j, g):
            if g < 2:
                return ("rz", j // 2), (j % 2) * 2 + g
            return ("n", j // 4), j % 4

        def turn(kind, u):
            banks = []
            for hb in range(2):
                pt = psum.tile([P, 2, 2, P], F32, name="tp", tag="tp", bufs=TP_BUFS)
                for a in range(2):
                    for w in range(2):
                        nc.tensor.transpose(pt[:, a, w, :], source(kind, u, 2 * hb + a)[:, w:I // 2:2], ident_f[:])
                banks.append(pt)
            turned[(kind, u)] = banks

        def gather(kind, u, hb, eng):
            if hb == 0:
                grouped[(kind, u)] = stage.tile([P, 4 * I], BF16, name="grouped", tag="grouped", align_bytes=64)
            g_ = grouped[(kind, u)]
            dst = g_[:, 2 * I * hb:2 * I * (hb + 1)].bitcast(F32).rearrange("p (a r w) -> p a r w", a=2, w=2)
            src = turned[(kind, u)][hb][:].rearrange("p a w r -> p a r w")
            copy(eng, dst, src)

        def quant(kind, u, halves):
            key = (kind, u)
            if key not in codes:
                name = "%s%d" % key
                codes[key] = const.tile([P, 4 * P], U32, name="codes_" + name, tag="codes_" + name, align_bytes=64)
                scales[key] = const.tile([P, 4 * P], U8, name="scales_" + name, tag="scales_" + name, align_bytes=64)
            lo, hi = 2 * P * halves[0], 2 * P * (halves[-1] + 1)
            nc.vector.quantize_mx(
                out=codes[key][:, lo:hi].bitcast(FP8X4), scales=scales[key][:, lo:hi], in_=grouped[key][:, 4 * lo:4 * hi]
            )

        gh_ps = {}
        ghT = {}
        for kind in ("r", "z", "n"):
            ghT[kind] = const.tile([P, NJ, 1, P], F32, name="ghT_" + kind, tag="ghT_" + kind)
        bias = const.tile([P, 24, 1], F32, name="bias", tag="bias")
        b_ps = {}

        def gh_turn(kind, u):
            if kind == "z":
                pt = psum.tile([P, 4, P], F32, name="tp", tag="tp", bufs=TP_BUFS)
                for c in range(4):
                    row = NJ + 4 * u + c
                    nc.tensor.matmul(out=pt[:, c, :], lhsT=ident_b[:], rhs=gh_raw[u][:, 1, c, :], start=True, stop=False)
                    nc.tensor.matmul(
                        out=pt[:, c, :], lhsT=ident_b[:, row:row + 1].to_broadcast([P, P]), rhs=b_rows[:],
                        start=False, stop=True,
                    )
            else:
                pt = psum.tile([P, 4, P], BF16, name="tp", tag="tp", bufs=TP_BUFS)
                for c in range(4):
                    nc.tensor.transpose(pt[:, c, :], gh_raw[u][:, 0 if kind == "r" else 2, c, :], ident_b[:])
            gh_ps[(kind, u)] = pt

        def gh_gather(kind, u, eng):
            dst = ghT[kind][:, 4 * u:4 * u + 4, 0, :]
            if kind == "r":
                nc.vector.tensor_tensor(
                    out=dst, in0=gh_ps[(kind, u)][:], in1=bias[:, 4 * u:4 * u + 4, :].to_broadcast([P, 4, P]), op=ALU.add
                )
            else:
                copy(eng, dst, gh_ps[(kind, u)][:])

        def bias_turn():
            pt = psum.tile([P, P], BF16, name="tp", tag="tp", bufs=TP_BUFS)
            nc.tensor.transpose(pt[:], b_rows[:], ident_b[:])
            b_ps[0] = pt

        def bias_gather():
            nc.vector.tensor_copy(out=bias[:, :, 0], in_=b_ps[0][:, 0:24])

        acc = {}
        sb = {}
        o_t = {}
        f8_t = {}
        part = {}
        rs_t = {}

        def steps(K):
            return list(enumerate(chunks[K])) if 0 <= K < NC else []

        def mm(K, g, only=None):
            for pos, (tg, j) in steps(K):
                if only is not None and pos != only:
                    continue
                key, c = where(j, g)
                tag = "acc%d" % g
                ps = psum.tile([P, TG, P], F32, name=tag, tag=tag, bufs=(R_BUFS, Z_BUFS, N_BUFS)[g])
                cols = slice(c * P, (c + 1) * P)
                if g == 1:
                    for t in range(TG):
                        rows = slice(t * P, (t + 1) * P)
                        nc.tensor.matmul_mx(
                            out=ps[:, t, :],
                            lhsT=codes[("x", tg)][:, rows].bitcast(FP8X4),
                            lhsT_scale=scales[("x", tg)][:, rows],
                            rhs=codes[key][:, cols].bitcast(FP8X4),
                            rhs_scale=scales[key][:, cols],
                            start=True,
                            stop=True,
                        )
                else:
                    nc.tensor.matmul_mx(
                        out=ps[:].rearrange("p t b -> p (t b)"),
                        lhsT=codes[key][:, cols].bitcast(FP8X4),
                        lhsT_scale=scales[key][:, cols],
                        rhs=codes[("x", tg)][:].bitcast(FP8X4),
                        rhs_scale=scales[("x", tg)][:],
                        start=True,
                        stop=True,
                    )
                acc[(K, pos, g)] = ps

        def wide(what, K, bufs):
            if (what, K) not in sb:
                sb[(what, K)] = work.tile([P, 2, TG, P], F32, name=what, tag=what, bufs=bufs)
            return sb[(what, K)]

        def add_gh(K, pos, g):
            tg, j = chunks[K][pos]
            kind = ("r", "z")[g]
            t_ = wide("a" + kind, K, 2)
            nc.vector.tensor_tensor(
                out=t_[:, pos], in0=acc[(K, pos, g)][:], in1=ghT[kind][:, j, :, :].to_broadcast([P, TG, P]), op=ALU.add
            )

        def sig(K, kind):
            if not steps(K):
                return
            n = len(chunks[K])
            t_ = wide(kind, K, 3 if kind == "z" else 2)
            nc.scalar.activation(
                out=t_[:, 0:n], in_=sb[("a" + kind, K)][:, 0:n], func=ACT.Sigmoid, scale=(1.0 if kind == "r" else -1.0)
            )

        def mul_m(K):
            if not steps(K):
                return
            ch = chunks[K]
            n = len(ch)
            t_ = wide("m", K, 3)
            if n == 2 and ch[0][1] != ch[1][1]:
                in1 = ghT["n"][:, ch[0][1]:ch[0][1] + 2, :, :].to_broadcast([P, 2, TG, P])
            else:
                in1 = ghT["n"][:, ch[0][1]:ch[0][1] + 1, :, :].to_broadcast([P, n, TG, P])
            nc.gpsimd.tensor_tensor(out=t_[:, 0:n], in0=sb[("r", K)][:, 0:n], in1=in1, op=ALU.mult)

        def add_n(K, pos):
            tg, j = chunks[K][pos]
            t_ = work.tile([P, TG, P], F32, name="np", tag="np", bufs=3)
            nc.vector.scalar_tensor_tensor(
                out=t_[:], in0=acc[(K, pos, 2)][:], scalar=bias[:, 2 * NJ + j, :], in1=sb[("m", K)][:, pos],
                op0=ALU.add, op1=ALU.add,
            )
            sb[("np", K, pos)] = t_

        def turn_np(K, pos):
            pt = psum.tile([P, TG, P], F32, name="tp", tag="tp", bufs=TP_BUFS)
            for t in range(TG):
                nc.tensor.transpose(pt[:, t, :], sb[("np", K, pos)][:, t, :], ident_f[:])
            acc[(K, pos, 3)] = pt

        def gate_n(K, pos):
            t_ = wide("n", K, 2)
            nc.scalar.activation(out=t_[:, pos], in_=acc[(K, pos, 3)][:], func=ACT.Tanh)

        done = {}

        def mul_h(K):
            if not steps(K):
                return
            ch = chunks[K]
            n = len(ch)
            tg, j = ch[0]
            hf = tg // 2
            if hf not in o_t:
                o_t[hf] = const.tile([P, 2 * TG, H], F32, name="o%d" % hf, tag="o%d" % hf)
            row = TG * (tg % 2)
            zc, n_ = sb[("z", K)], sb[("n", K)]
            if n == 2 and ch[1][0] != tg:
                dst = o_t[hf][:, :, j * P:(j + 1) * P]
                nc.gpsimd.tensor_tensor(
                    out=dst, in0=zc[:].rearrange("p n t c -> p (n t) c"), in1=n_[:].rearrange("p n t c -> p (n t) c"), op=ALU.mult
                )
            elif n == 2:
                dst = o_t[hf][:, row:row + TG, j * P:(j + 2) * P].rearrange("p t (n c) -> p n t c", n=2)
                nc.gpsimd.tensor_tensor(out=dst, in0=zc[:], in1=n_[:], op=ALU.mult)
            else:
                dst = o_t[hf][:, row:row + TG, j * P:(j + 1) * P]
                nc.gpsimd.tensor_tensor(out=dst, in0=zc[:, 0], in1=n_[:, 0], op=ALU.mult)
            for tg_, j_ in ch:
                done[tg_] = done.get(tg_, 0) + 1
                bd = bounds(tg_)
                cols = done[tg_] * P
                if tg_ == NTG - 1:
                    if cols in bd:
                        store_o(tg_, bd[bd.index(cols) - 1], cols)
                elif cols == H:
                    store_o(tg_, 0, H)

        def rows_of(tg):
            return o_t[tg // 2][:, TG * (tg % 2):TG * (tg % 2) + TG, :]

        def bounds(tg):
            if tg == NTG - 1:
                return [0, 512, 768, 896, 1024]
            return [0, 512, 1024]

        def amax_piece(tg, s, t):
            bd = bounds(tg)
            if tg not in part:
                part[tg] = const.tile([P, TG, len(bd) - 1], F32, name="part%d" % tg, tag="part%d" % tg)
            nc.vector.tensor_reduce(
                out=part[tg][:, t, s:s + 1], in_=rows_of(tg)[:, t, bd[s]:bd[s + 1]], axis=AX.X, op=ALU.max,
                apply_absolute_value=True,
            )

        def combine(tg):
            am = const.tile([P, TG], F32, name="am%d" % tg, tag="am%d" % tg)
            rc = const.tile([P, TG], F32, name="rc%d" % tg, tag="rc%d" % tg)
            rs = const.tile([P, TG], F32, name="rs%d" % tg, tag="rs%d" % tg)
            nc.vector.tensor_reduce(out=am[:], in_=part[tg][:], axis=AX.X, op=ALU.max)
            nc.vector.reciprocal(out=rc[:], in_=am[:])
            nc.vector.tensor_scalar(out=rs[:], in0=rc[:], scalar1=448.0, scalar2=None, op0=ALU.mult)
            rs_t[tg] = rs
            f8_t[tg] = const.tile([P, TG, H], FP8, name="f8_%d" % tg, tag="f8_%d" % tg)

        def cast_piece(tg, t, c0, c1, eng):
            if eng == "s":
                nc.scalar.activation(
                    out=f8_t[tg][:, t, c0:c1], in_=rows_of(tg)[:, t, c0:c1], func=ACT.Identity,
                    scale=rs_t[tg][:, t:t + 1], bias=zero[:, 0:1], saturate=False,
                )
            else:
                nc.vector.tensor_scalar(
                    out=f8_t[tg][:, t, c0:c1], in0=rows_of(tg)[:, t, c0:c1], scalar1=rs_t[tg][:, t:t + 1],
                    scalar2=None, op0=ALU.mult, saturate=False,
                )

        def store_o(tg, c0, c1):
            nc.sync.dma_start(out=out_0[:, TG * tg:TG * (tg + 1), c0:c1], in_=rows_of(tg)[:, :, c0:c1])

        def store_f8(tg, t0, t1):
            nc.sync.dma_start(out=out_1[:, TG * tg + t0:TG * tg + t1, :], in_=f8_t[tg][:, t0:t1, :].bitcast(U8))

        flat = []
        for K in range(NC):
            for pos in range(len(chunks[K])):
                flat.append((K, pos))
        NS = len(flat)

        def ok(i):
            return 0 <= i < NS

        def last(i):
            return ok(i) and flat[i][1] == len(chunks[flat[i][0]]) - 1

        first_use = {}
        h_iter = {}
        cnt = {}
        for i in range(NS):
            K, pos = flat[i]
            tg, j = chunks[K][pos]
            for key in (("x", tg), ("rz", j // 2), ("n", j // 4), ("gr", j // 4), ("gz", j // 4), ("gn", j // 4)):
                first_use.setdefault(key, i)
            cnt[tg] = cnt.get(tg, 0) + P
            h_iter[(tg, cnt[tg])] = i + (len(chunks[K]) - 1 - pos) + D1 + 1
        LAST = NS + D1

        tasks = []
        count = {"n": 0}
        left = {}
        load_now = {"v": 0.0, "s": 0.0}
        credit = {"v": 0.0, "s": 0.0}

        def queue(due, ready, what, *args):
            count["n"] += 1
            tasks.append([due, count["n"], ready, what, args])

        for tg in range(NTG):
            bd = bounds(tg)
            left[("amax", tg)] = TG * (len(bd) - 1)
            for s in range(len(bd) - 1):
                ready = min(h_iter[(tg, bd[s + 1])] + AMAX_LAG, LAST)
                for t in range(TG):
                    queue(ready + (0 if tg == NTG - 1 else AMAX_SLACK), ready, "amax", tg, s, t)

        def cost_of(what, args, eng):
            if what == "amax":
                bd = bounds(args[0])
                return (bd[args[1] + 1] - bd[args[1]]) / 512.0
            if what == "combine":
                return 0.5
            if what == "cast":
                return (args[3] - args[2]) / (1024.0 if eng == "v" else 512.0)
            return 1.0

        def engines_of(what, args, i):
            if what in ("amax", "combine", "quant") or (what == "ghg" and args[0] == "r"):
                return ["v"]
            if what == "cast":
                return ["s", "v"] if i >= LAST else ["s"]
            if what == "gather":
                return ["s"] if i >= 2 else ["s", "v"]
            return ["s", "v"]

        def emit(what, args, eng, i):
            nxt = i if i >= LAST else i + 1
            if what == "gather":
                kind, u, hb, due = args
                gather(kind, u, hb, eng)
                left[(kind, u)] -= 1
                if left[(kind, u)] == 0:
                    queue(max(due, i + 1), i + 1, "quant", kind, u)
            elif what == "quant":
                quant(args[0], args[1], [0, 1])
            elif what == "ghg":
                gh_gather(args[0], args[1], eng)
            elif what == "amax":
                amax_piece(*args)
                tg = args[0]
                left[("amax", tg)] -= 1
                if left[("amax", tg)] == 0:
                    queue(nxt, nxt, "combine", tg)
            elif what == "combine":
                tg = args[0]
                combine(tg)
                for t in range(TG):
                    if tg == NTG - 1:
                        queue(nxt, nxt, "cast", tg, t, 0, 512)
                        queue(nxt, nxt, "cast", tg, t, 512, H)
                    else:
                        queue(nxt + CAST_SLACK, nxt, "cast", tg, t, 0, H)
            elif what == "cast":
                tg, t, c0, c1 = args
                cast_piece(tg, t, c0, c1, eng)
                if c1 == H:
                    if tg >= NTG - 2:
                        store_f8(tg, t, t + 1)
                    elif t == TG - 1:
                        store_f8(tg, 0, TG)

        def side(i):
            budget = {"v": BUDGET_V, "s": BUDGET_S}
            if i >= NS:
                budget = {"v": DRAIN_V, "s": DRAIN_S}
            if i >= LAST:
                budget = {"v": 100.0, "s": 100.0}
            again = True
            while again:
                again = False
                for task in sorted(tasks, key=lambda task: (task[0] if i < LAST else 0, task[1])):
                    due, number, ready, what, args = task
                    if ready > i:
                        continue
                    best = None
                    for eng in engines_of(what, args, i):
                        over = load_now[eng] + cost_of(what, args, eng) - budget[eng] - credit[eng]
                        if best is None or over < best[0]:
                            best = (over, eng)
                    if best[0] > 0 and due > i:
                        continue
                    tasks.remove(task)
                    load_now[best[1]] += cost_of(what, args, best[1])
                    emit(what, args, best[1], i)
                    again = True
                    break
            for eng in ("v", "s"):
                credit[eng] = max(-2.0, min(2.0, credit[eng] + budget[eng] - load_now[eng]))

        lag = {"x": -1, "rz": -1, "n": D1 - 1, "gr": -1, "gz": DZ - 1, "gn": -1}
        need = {}
        for key in first_use:
            need[key] = first_use[key] + lag[key[0]]
        units = sorted(
            [key for key in first_use if key not in (("x", 0), ("rz", 0), ("gr", 0), ("gz", 0), ("gn", 0))],
            key=lambda key: (need[key], key),
        )

        def turns(i):
            big = 0
            small = 0
            for key in list(units):
                is_gh = key[0] in ("gr", "gz", "gn")
                forced = need[key] - (1 if is_gh else 2) <= i
                if not forced and (need[key] - LEAD > i or (small if is_gh else big)):
                    continue
                units.remove(key)
                if is_gh:
                    small += 1
                    gh_turn(key[0][1], key[1])
                    queue(i + 1, i + 1, "ghg", key[0][1], key[1])
                else:
                    big += 1
                    turn(key[0], key[1])
                    if key == ("x", 1):
                        load_x(3)
                    left[key] = 2
                    queue(i + 1, i + 1, "gather", key[0], key[1], 0, max(i + 1, need[key]))
                    queue(i + 1, i + 1, "gather", key[0], key[1], 1, max(i + 1, need[key]))

        turn("x", 0)
        load_x(2)
        turn("rz", 0)
        gather("x", 0, 0, "v")
        gather("x", 0, 1, "s")
        gather("rz", 0, 0, "s")
        quant("x", 0, [0, 1])
        gather("rz", 0, 1, "s")
        bias_turn()
        gh_turn("r", 0)
        gh_turn("n", 0)
        quant("rz", 0, [0])
        bias_gather()
        gh_gather("r", 0, "v")
        gh_gather("n", 0, "s")
        gh_turn("z", 0)
        quant("rz", 0, [1])
        gh_gather("z", 0, "s")

        def at(i, fn, *a):
            if ok(i):
                fn(flat[i][0], flat[i][1], *a)

        def mm1(K, pos, g):
            mm(K, g, pos)

        i = -1
        while i < LAST + 1 or tasks:
            load_now["v"] = 1.0 * (ok(i) + ok(i - DZ) + ok(i - D1))
            load_now["s"] = 1.0 * ok(i - D1 - 1)
            for e in (i, i - DZ):
                if last(e):
                    load_now["s"] += len(chunks[flat[e][0]])
            at(i - D1 - 1, gate_n)
            if last(i - D1 - 1):
                mul_h(flat[i - D1 - 1][0])
            at(i, add_gh, 0)
            if last(i):
                sig(flat[i][0], "r")
                mul_m(flat[i][0])
            at(i - DZ, add_gh, 1)
            if last(i - DZ):
                sig(flat[i - DZ][0], "z")
            at(i - D1, add_n)
            side(i)
            at(i + 1, mm1, 0)
            at(i - DZ + 1, mm1, 1)
            at(i - D1 + 1, mm1, 2)
            at(i - D1, turn_np)
            turns(i)
            i += 1
